import numpy as np
import ml_dtypes


def mxq(x, axis, fmt="e4m3"):
    dtype, down = {"e4m3": (ml_dtypes.float8_e4m3fn, 7), "e5m2": (ml_dtypes.float8_e5m2, 14)}[fmt]
    v = np.moveaxis(np.asarray(x, np.float32).astype(ml_dtypes.bfloat16).astype(np.float64), axis, -1)
    blocks = v.reshape(v.shape[:-1] + (-1, 32))
    amax = np.abs(blocks).max(-1, keepdims=True)
    byte = np.maximum(np.where(amax > 0, np.frexp(amax)[1] - 1 + 127, 0) - down, 1)
    scale = np.exp2(byte - 127.0)
    codes = (blocks / scale).astype(np.float32).astype(dtype).astype(np.float64)
    return np.moveaxis((codes * scale).reshape(v.shape), -1, axis)


WIDE = False


def mx_kscale(k):
    if not WIDE:
        return np.ones(k)
    levels = np.array([10, -10, 5, -5, 0])
    if k % 512:
        return np.exp2(np.random.permutation(np.resize(levels, k // 32))).repeat(32)
    a = np.empty((k // 512, 16))
    for p in range(k // 512):
        a[p, :8] = np.random.permutation(np.resize(levels, 8))
        for g in range(8):
            far = levels[np.abs(levels - a[p, g]) >= 10]
            a[p, g + 8] = far[np.random.randint(len(far))]
    return np.exp2(a.ravel()).repeat(32)


BF16 = ml_dtypes.bfloat16


def bf(x):
    return np.asarray(x, np.float32).astype(BF16)


def f64(x):
    return np.asarray(x).astype(np.float64)


N, E, C, D1, D2 = 16384, 512, 128, 2, 2
T1 = D1 + 1


def shift_down(y, k):
    return np.pad(y, ((k, 0), (0, 0)))[:y.shape[0]] if k > 0 else y


def setup_inputs():
    s = mx_kscale(E)
    return {"x": bf(np.random.standard_normal((N, E)) * s),
            "W1": bf(np.random.standard_normal((T1, E, C)) * 0.4 / np.sqrt(E) / s[None, :, None]),
            "b1": bf(np.random.standard_normal((1, C)) * 0.25)}


def reference(x, W1, b1):
    Y = mxq(f64(x), 1, "e4m3") @ mxq(f64(W1), 1, "e4m3")
    S = sum(shift_down(Y[k], k) for k in range(T1))
    cnt1 = np.minimum(np.arange(N), D1) + 1.0
    return np.tanh(S + cnt1[:, None] * f64(b1)[0])

@@ -1,0 +1,232 @@
+from contextlib import ExitStack
+
+import concourse.mybir as mybir
+from concourse.masks import make_identity
+
+F32 = mybir.dt.float32
+BF16 = mybir.dt.bfloat16
+U32 = mybir.dt.uint32
+U8 = mybir.dt.uint8
+FP8X4 = mybir.dt.float8_e4m3fn_x4
+ADD = mybir.AluOpType.add
+TANH = mybir.ActivationFunctionType.Tanh
+
+P = 128
+N_ROWS = 16384
+E = 512
+C = 128
+TAPS = 3
+R = N_ROWS // P
+WORDS = E // 2
+FLOPS = 2 * N_ROWS * E * C * TAPS
+
+LEAD = 17
+UNITS = [(-2, 2), (0, 4), (4, 4)] + [(r, 8) for r in range(8, R, 8)]
+LOADS = [(R - 2, 2), (0, 4), (4, 4)] + [(r, 8) for r in range(8, R - 8, 8)] + [(R - 8, 6)]
+VECTOR_EXITS = {1: (), 2: (1,), 4: (3,), 8: (1, 3)}
+
+
+def tile_predictor_pa_t_kernel(tc, x, W1, b1, out):
+    nc = tc.nc
+    xv = x.rearrange("(j r) k -> j (r k)", r=R)
+    ov = out.rearrange("(j r) c -> j (r c)", r=R)
+    with ExitStack() as ctx:
+        const = ctx.enter_context(tc.tile_pool(name="const", bufs=1))
+        rawp = ctx.enter_context(tc.tile_pool(name="raw", bufs=1))
+        grp = ctx.enter_context(tc.tile_pool(name="grouped", bufs=4))
+        qp = ctx.enter_context(tc.tile_pool(name="quant", bufs=8))
+        outp = ctx.enter_context(tc.tile_pool(name="outs", bufs=12))
+        psum = ctx.enter_context(tc.psum_pool(name="psum", bufs=1))
+        ctx.enter_context(tc.manual_schedule())
+
+        raw_of = {}
+        blk = {}
+        state = {"a": 0, "b": 0, "load": 0}
+
+        def load_next():
+            if state["load"] >= len(LOADS):
+                return
+            r0, nb = LOADS[state["load"]]
+            if state["load"] == 0:
+                t = const.tile([P, nb * E], BF16, name="rawh")
+            else:
+                t = rawp.tile([P, nb * E], BF16, name="raw%d" % r0)
+            state["load"] += 1
+            nc.sync.dma_start(out=t[:], in_=xv[:, r0 * E:(r0 + nb) * E])
+            for b in range(nb):
+                raw_of[r0 + b] = (t, b)
+
+        def psum_bank(kind):
+            t = psum.tile([P, 512], F32, tag="%s%d" % (kind, state[kind] % 4), name="p%s%d" % (kind, state[kind]))
+            state[kind] += 1
+            return t
+
+        ident = const.tile([P, P], F32, name="ident")
+        make_identity(nc, ident[:])
+        warm = const.tile([P, 1], F32, name="warm")
+        nc.vector.memset(warm[:], 0.0)
+        nc.scalar.activation(out=warm[:], in_=warm[:], func=TANH)
+        bz = const.tile([P, C], BF16, name="bz")
+        nc.vector.memset(bz[:], 0.0)
+        nc.scalar.dma_start(out=bz[0:1, :], in_=b1)
+        coef = const.tile([P, TAPS, P], BF16, name="coef")
+        nc.vector.memset(coef[:], 3.0)
+        nc.vector.memset(coef[0:1, 0, 0:1], 1.0)
+        nc.vector.memset(coef[0:1, 1, 0:1], 2.0)
+        shift = const.tile([P, P], F32, name="shift")
+        nc.vector.memset(shift[:], 0.0)
+        nc.vector.tensor_copy(out=shift[:, 1:P], in_=ident[:, 0:P - 1])
+
+        load_next()
+        wraw = const.tile([P, TAPS, 4, C], BF16, name="wraw")
+        nc.sync.dma_start(
+            out=wraw[:].rearrange("p k (u e) c -> p k u (e c)", u=2),
+            in_=W1.rearrange("k (p u e) c -> p k u (e c)", u=2, p=P, e=2),
+        )
+        for i in range(LEAD):
+            load_next()
+
+        wg = const.tile([P, TAPS, C, 4], BF16, name="wg", align_bytes=64)
+        wq = const.tile([P, TAPS * C], U32, name="wq", align_bytes=64)
+        ws = const.tile([P, TAPS * C], U8, name="ws", align_bytes=64)
+        bias = const.tile([P, TAPS, C], F32, name="bias")
+
+        def prepare_w():
+            nc.vector.tensor_copy(out=wg[:], in_=wraw[:].rearrange("p k t c -> p k c t"))
+            for k in range(TAPS):
+                nc.vector.quantize_mx(
+                    out=wq[:, k * C:(k + 1) * C].bitcast(FP8X4),
+                    scales=ws[:, k * C:(k + 1) * C],
+                    in_=wg[:, k].rearrange("p c t -> p (c t)"),
+                )
+
+        def transpose_and_leave(u):
+            r0, nb = UNITS[u]
+            fills = nb // 2
+            gs = []
+            for first in range(0, fills, 4):
+                group = list(range(first, min(first + 4, fills)))
+                pas = {}
+                for h in group:
+                    pa = psum_bank("a")
+                    pas[h] = pa
+                    for b in range(2):
+                        r = r0 + 2 * h + b
+                        t, i = raw_of[r % R]
+                        words = t[:].bitcast(F32)
+                        for v in range(2):
+                            lo = i * WORDS + v
+                            nc.tensor.transpose(
+                                pa[:, (2 * b + v) * P:(2 * b + v + 1) * P],
+                                words[:, lo:(i + 1) * WORDS:2],
+                                (shift if r < 0 else ident)[:],
+                            )
+                for h in group:
+                    if h % 2 == 0:
+                        g = grp.tile([P, min(nb, 4) * 2 * P], F32, tag="g", name="g%d_%d" % (u, h), align_bytes=64)
+                        gs.append(g)
+                    dst = gs[-1][:, (h % 2) * 512:(h % 2 + 1) * 512].rearrange("p (b j v) -> p b j v", b=2, v=2)
+                    src = pas[h][:].rearrange("p (b v j) -> p b j v", b=2, v=2)
+                    if h in VECTOR_EXITS[fills]:
+                        nc.vector.tensor_copy(out=dst, in_=src)
+                    else:
+                        nc.scalar.copy(out=dst, in_=src)
+            return gs
+
+        def quantise(u, n, g):
+            r0, nb = UNITS[u]
+            w = min(nb, 4)
+            cq = qp.tile([P, w * P], U32, tag="cq", name="cq%d_%d" % (u, n), align_bytes=64)
+            sq = qp.tile([P, w * P], U8, tag="sq", name="sq%d_%d" % (u, n), align_bytes=64)
+            nc.vector.quantize_mx(out=cq[:].bitcast(FP8X4), scales=sq[:], in_=g[:].bitcast(BF16))
+            for b in range(w):
+                blk[r0 + 4 * n + b] = (cq, sq, b)
+
+        def multiply(u, sizes):
+            r0, nb = UNITS[u]
+            banks = []
+            r = r0
+            for n, size in enumerate(sizes):
+                pb = psum_bank("b" if n < 4 else "a")
+                passes = [(r + h, 0, 2, h) for h in range(0, size, 2)]
+                passes += [(r + h - 1, 1, 2, h) for h in range(0, size, 2)]
+                for h in range(0, size, 2):
+                    passes += [(r + h - 2, 2, 1, h), (r + h + 1, 0, 1, h + 1)]
+                for m, (s, k, nk, ob) in enumerate(passes):
+                    cq, sq, i = blk[s]
+                    nc.tensor.matmul_mx(
+                        out=pb[:, ob * C:(ob + nk) * C],
+                        lhsT=cq[:, i * P:(i + 1) * P].bitcast(FP8X4),
+                        lhsT_scale=sq[:, i * P:(i + 1) * P],
+                        rhs=wq[:, k * C:(k + nk) * C].bitcast(FP8X4),
+                        rhs_scale=ws[:, k * C:(k + nk) * C],
+                        start=(m == 0),
+                        stop=(m == len(passes) - 1),
+                    )
+                banks.append((pb, r, size))
+                r += size
+            return banks
+
+        o_of = {}
+
+        def add_bias(pb, r, size):
+            if r % 8 == 0 or r not in o_of:
+                o = outp.tile([P, 8 * C], F32, tag="o", name="o%d" % r)
+                for b in range(8):
+                    o_of[r + b] = (o, b)
+            o, b = o_of[r]
+            ob = o[:, b * C:(b + size) * C].rearrange("p (n c) -> p n c", c=C)
+            pv = pb[:, 0:size * C].rearrange("p (n c) -> p n c", c=C)
+            if r == 0:
+                nc.vector.tensor_tensor(out=ob[:, 0:3, :], in0=pv[:, 0:3, :], in1=bias[:], op=ADD)
+                nc.vector.tensor_tensor(out=ob[:, 3, :], in0=pv[:, 3, :], in1=bias[:, 2, :], op=ADD)
+            else:
+                nc.vector.tensor_tensor(out=ob, in0=pv, in1=bias[:, 2:3, :].to_broadcast([P, size, C]), op=ADD)
+
+        def tanh_store(r, size):
+            o, b = o_of[r]
+            nc.scalar.activation(out=o[:, b * C:(b + size) * C], in_=o[:, b * C:(b + size) * C], func=TANH)
+            nc.sync.dma_start(out=ov[:, r * C:(r + size) * C], in_=o[:, b * C:(b + size) * C])
+
+        n_units = len(UNITS)
+        for p in range(n_units + 1):
+            last = p == n_units
+            late = []
+            if not last:
+                gs = transpose_and_leave(p)
+                if p == 0:
+                    prepare_w()
+                if p == 1:
+                    pbias = psum.tile([P, TAPS, C], F32, tag="b3", name="pbias")
+                    for k in range(TAPS):
+                        nc.tensor.matmul(out=pbias[:, k, :], lhsT=coef[:, k, :], rhs=bz[:], start=True, stop=True)
+                for n, g in enumerate(gs):
+                    if n == 3:
+                        late.append((n, g))
+                    else:
+                        quantise(p, n, g)
+                if p == 1:
+                    nc.vector.tensor_copy(out=bias[:], in_=pbias[:])
+            banks = []
+            if p >= 2:
+                nb = UNITS[p - 1][1]
+                banks = multiply(p - 1, [4, 2, 2] if last else [4] * (nb // 4))
+            if not last:
+                for n, (pb, r, size) in enumerate(banks):
+                    add_bias(pb, r, size)
+                    if n == 0:
+                        for m, g in late:
+                            quantise(p, m, g)
+                        late = []
+                for m, g in late:
+                    quantise(p, m, g)
+            if p >= 3:
+                r0, nb = UNITS[p - 2]
+                piece = 4 if last else min(nb, 8)
+                for r in range(r0, r0 + nb, piece):
+                    tanh_store(r, piece)
+                    load_next()
+            if last:
+                for pb, r, size in banks:
+                    add_bias(pb, r, size)
+                    tanh_store(r, size)

@@ -23,7 +23,8 @@ FLOPS = 2 * N_ROWS * E * C * TAPS
 LEAD = 17
 UNITS = [(-2, 2), (0, 4), (4, 4)] + [(r, 8) for r in range(8, R, 8)]
 LOADS = [(R - 2, 2), (0, 4), (4, 4)] + [(r, 8) for r in range(8, R - 8, 8)] + [(R - 8, 6)]
-VECTOR_EXITS = {1: (), 2: (1,), 4: (3,), 8: (1, 3)}
+VECTOR_EXITS = {1: (), 2: (1,), 4: ()}
+ORDERED = 6
 
 
 def tile_predictor_pa_t_kernel(tc, x, W1, b1, out):
@@ -33,9 +34,10 @@ def tile_predictor_pa_t_kernel(tc, x, W1, b1, out):
     with ExitStack() as ctx:
         const = ctx.enter_context(tc.tile_pool(name="const", bufs=1))
         rawp = ctx.enter_context(tc.tile_pool(name="raw", bufs=1))
+        ordp = ctx.enter_context(tc.tile_pool(name="ordered", bufs=2))
         grp = ctx.enter_context(tc.tile_pool(name="grouped", bufs=4))
         qp = ctx.enter_context(tc.tile_pool(name="quant", bufs=8))
-        outp = ctx.enter_context(tc.tile_pool(name="outs", bufs=12))
+        outp = ctx.enter_context(tc.tile_pool(name="outs", bufs=10))
         psum = ctx.enter_context(tc.psum_pool(name="psum", bufs=1))
         ctx.enter_context(tc.manual_schedule())
 
@@ -100,6 +102,29 @@ def tile_predictor_pa_t_kernel(tc, x, W1, b1, out):
                     in_=wg[:, k].rearrange("p c t -> p (c t)"),
                 )
 
+        ordered = {}
+
+        def order_words(u):
+            r0, nb = UNITS[u]
+            if nb < 8:
+                return
+            t, i = raw_of[r0]
+            xo = ordp.tile([P, ORDERED * E], BF16, tag="xo", name="xo%d" % u)
+            nc.vector.tensor_copy(
+                out=xo[:].bitcast(F32).rearrange("p (v n) -> p v n", v=2),
+                in_=t[:, i * E:(i + ORDERED) * E].bitcast(F32).rearrange("p (n v) -> p v n", v=2),
+            )
+            for b in range(ORDERED):
+                ordered[r0 + b] = (xo, b)
+
+        def window(r, v):
+            if r in ordered:
+                xo, b = ordered[r]
+                lo = (v * ORDERED + b) * P
+                return xo[:].bitcast(F32)[:, lo:lo + P]
+            t, i = raw_of[r % R]
+            return t[:].bitcast(F32)[:, i * WORDS + v:(i + 1) * WORDS:2]
+
         def transpose_and_leave(u):
             r0, nb = UNITS[u]
             fills = nb // 2
@@ -112,13 +137,10 @@ def tile_predictor_pa_t_kernel(tc, x, W1, b1, out):
                     pas[h] = pa
                     for b in range(2):
                         r = r0 + 2 * h + b
-                        t, i = raw_of[r % R]
-                        words = t[:].bitcast(F32)
                         for v in range(2):
-                            lo = i * WORDS + v
                             nc.tensor.transpose(
                                 pa[:, (2 * b + v) * P:(2 * b + v + 1) * P],
-                                words[:, lo:(i + 1) * WORDS:2],
+                                window(r, v),
                                 (shift if r < 0 else ident)[:],
                             )
                 for h in group:
@@ -193,6 +215,8 @@ def tile_predictor_pa_t_kernel(tc, x, W1, b1, out):
             last = p == n_units
             late = []
             if not last:
+                if p + 1 < n_units:
+                    order_words(p + 1)
                 gs = transpose_and_leave(p)
                 if p == 0:
                     prepare_w()

@@ -20,11 +20,8 @@ R = N_ROWS // P
 WORDS = E // 2
 FLOPS = 2 * N_ROWS * E * C * TAPS
 
-LEAD = 17
 UNITS = [(-2, 2), (0, 4), (4, 4)] + [(r, 8) for r in range(8, R, 8)]
 LOADS = [(R - 2, 2), (0, 4), (4, 4)] + [(r, 8) for r in range(8, R - 8, 8)] + [(R - 8, 6)]
-VECTOR_EXITS = {1: (), 2: (1,), 4: ()}
-ORDERED = 6
 
 
 def tile_predictor_pa_t_kernel(tc, x, W1, b1, out):
@@ -34,10 +31,10 @@ def tile_predictor_pa_t_kernel(tc, x, W1, b1, out):
     with ExitStack() as ctx:
         const = ctx.enter_context(tc.tile_pool(name="const", bufs=1))
         rawp = ctx.enter_context(tc.tile_pool(name="raw", bufs=1))
-        ordp = ctx.enter_context(tc.tile_pool(name="ordered", bufs=2))
+        tmpp = ctx.enter_context(tc.tile_pool(name="aside", bufs=2))
         grp = ctx.enter_context(tc.tile_pool(name="grouped", bufs=4))
         qp = ctx.enter_context(tc.tile_pool(name="quant", bufs=8))
-        outp = ctx.enter_context(tc.tile_pool(name="outs", bufs=10))
+        outp = ctx.enter_context(tc.tile_pool(name="outs", bufs=12))
         psum = ctx.enter_context(tc.psum_pool(name="psum", bufs=1))
         ctx.enter_context(tc.manual_schedule())
 
@@ -46,8 +43,6 @@ def tile_predictor_pa_t_kernel(tc, x, W1, b1, out):
         state = {"a": 0, "b": 0, "load": 0}
 
         def load_next():
-            if state["load"] >= len(LOADS):
-                return
             r0, nb = LOADS[state["load"]]
             if state["load"] == 0:
                 t = const.tile([P, nb * E], BF16, name="rawh")
@@ -85,82 +80,106 @@ def tile_predictor_pa_t_kernel(tc, x, W1, b1, out):
             out=wraw[:].rearrange("p k (u e) c -> p k u (e c)", u=2),
             in_=W1.rearrange("k (p u e) c -> p k u (e c)", u=2, p=P, e=2),
         )
-        for i in range(LEAD):
+        while state["load"] < len(LOADS):
             load_next()
+
+        perm = const.tile([P, 2, 2, P], BF16, name="perm")
+        nc.vector.memset(perm[:], 0.0)
+        for v in range(2):
+            for s in range(2):
+                nc.vector.tensor_copy(
+                    out=perm[:, v, s, :].rearrange("q (m h j z) -> q m h j z", m=8, h=2, z=2)[:, :, :, :, s],
+                    in_=ident[:].rearrange("q (h m v j) -> q m h v j", h=2, m=8, v=2)[:, :, :, v, :],
+                )
 
         wg = const.tile([P, TAPS, C, 4], BF16, name="wg", align_bytes=64)
         wq = const.tile([P, TAPS * C], U32, name="wq", align_bytes=64)
         ws = const.tile([P, TAPS * C], U8, name="ws", align_bytes=64)
         bias = const.tile([P, TAPS, C], F32, name="bias")
 
-        def prepare_w():
-            nc.vector.tensor_copy(out=wg[:], in_=wraw[:].rearrange("p k t c -> p k c t"))
-            for k in range(TAPS):
-                nc.vector.quantize_mx(
-                    out=wq[:, k * C:(k + 1) * C].bitcast(FP8X4),
-                    scales=ws[:, k * C:(k + 1) * C],
-                    in_=wg[:, k].rearrange("p c t -> p (c t)"),
-                )
+        def multiply_w(k):
+            pw = psum.tile([P, 4, C], F32, tag="b%d" % k, name="pw%d" % k)
+            for v in range(2):
+                for e in range(2):
+                    for s in range(2):
+                        nc.tensor.matmul(
+                            out=pw[:, 2 * v + e, :],
+                            lhsT=perm[:, v, s, :],
+                            rhs=wraw[:, k, 2 * s + e, :],
+                            start=(s == 0),
+                            stop=(s == 1),
+                        )
+            return pw
 
-        ordered = {}
-
-        def order_words(u):
-            r0, nb = UNITS[u]
-            if nb < 8:
-                return
-            t, i = raw_of[r0]
-            xo = ordp.tile([P, ORDERED * E], BF16, tag="xo", name="xo%d" % u)
-            nc.vector.tensor_copy(
-                out=xo[:].bitcast(F32).rearrange("p (v n) -> p v n", v=2),
-                in_=t[:, i * E:(i + ORDERED) * E].bitcast(F32).rearrange("p (n v) -> p v n", v=2),
+        def quantise_w(k):
+            nc.vector.quantize_mx(
+                out=wq[:, k * C:(k + 1) * C].bitcast(FP8X4),
+                scales=ws[:, k * C:(k + 1) * C],
+                in_=wg[:, k].rearrange("p c t -> p (c t)"),
             )
-            for b in range(ORDERED):
-                ordered[r0 + b] = (xo, b)
 
-        def window(r, v):
-            if r in ordered:
-                xo, b = ordered[r]
-                lo = (v * ORDERED + b) * P
-                return xo[:].bitcast(F32)[:, lo:lo + P]
-            t, i = raw_of[r % R]
-            return t[:].bitcast(F32)[:, i * WORDS + v:(i + 1) * WORDS:2]
+        done = set()
 
-        def transpose_and_leave(u):
+        def exchange(u):
             r0, nb = UNITS[u]
-            fills = nb // 2
-            gs = []
-            for first in range(0, fills, 4):
-                group = list(range(first, min(first + 4, fills)))
-                pas = {}
-                for h in group:
-                    pa = psum_bank("a")
-                    pas[h] = pa
-                    for b in range(2):
-                        r = r0 + 2 * h + b
-                        for v in range(2):
-                            nc.tensor.transpose(
-                                pa[:, (2 * b + v) * P:(2 * b + v + 1) * P],
-                                window(r, v),
-                                (shift if r < 0 else ident)[:],
-                            )
-                for h in group:
-                    if h % 2 == 0:
-                        g = grp.tile([P, min(nb, 4) * 2 * P], F32, tag="g", name="g%d_%d" % (u, h), align_bytes=64)
-                        gs.append(g)
-                    dst = gs[-1][:, (h % 2) * 512:(h % 2 + 1) * 512].rearrange("p (b j v) -> p b j v", b=2, v=2)
-                    src = pas[h][:].rearrange("p (b v j) -> p b j v", b=2, v=2)
-                    if h in VECTOR_EXITS[fills]:
-                        nc.vector.tensor_copy(out=dst, in_=src)
-                    else:
-                        nc.scalar.copy(out=dst, in_=src)
-            return gs
+            parts = []
+            for r in range(r0, r0 + nb):
+                t, i = raw_of[r % R]
+                if r % R in done:
+                    continue
+                done.add(r % R)
+                if parts and parts[-1][0] is t:
+                    parts[-1][2] += 1
+                else:
+                    parts.append([t, i, 1])
+            steps = [[], [], []]
+            for t, i, n in parts:
+                runs = t[:, i * E:(i + n) * E].bitcast(F32).rearrange("p (n h m v i) -> p n h m v i", h=2, m=8, v=2, i=8)
+                low, high = runs[:, :, 0, :, 1, :], runs[:, :, 1, :, 0, :]
+                aside = tmpp.tile([P, n, 8, 8], F32, tag="aside", name="aside%d_%d" % (u, i))
+                steps[0].append((aside[:], low))
+                steps[1].append((low, high))
+                steps[2].append((high, aside[:]))
 
-        def quantise(u, n, g):
+            def step(k):
+                for dst, src in steps[k]:
+                    nc.vector.tensor_copy(out=dst, in_=src)
+
+            return step
+
+        pas = {}
+        gs = {}
+
+        def transpose(u):
+            r0, nb = UNITS[u]
+            for h in range(nb // 2):
+                pa = psum_bank("a")
+                pas[u, h] = pa
+                for b in range(2):
+                    t, i = raw_of[(r0 + 2 * h + b) % R]
+                    for v in range(2):
+                        lo = i * WORDS + v * P
+                        nc.tensor.transpose(
+                            pa[:, (2 * b + v) * P:(2 * b + v + 1) * P],
+                            t[:].bitcast(F32)[:, lo:lo + P],
+                            (shift if r0 < 0 else ident)[:],
+                        )
+
+        def leave(u, h, copy):
+            nb = UNITS[u][1]
+            if h % 2 == 0:
+                gs[u, h // 2] = grp.tile([P, min(nb, 4) * 2 * P], F32, tag="g", name="g%d_%d" % (u, h), align_bytes=64)
+            copy(
+                out=gs[u, h // 2][:, (h % 2) * 512:(h % 2 + 1) * 512].rearrange("p (b j v) -> p b j v", b=2, v=2),
+                in_=pas[u, h][:].rearrange("p (b v j) -> p b j v", b=2, v=2),
+            )
+
+        def quantise(u, n):
             r0, nb = UNITS[u]
             w = min(nb, 4)
             cq = qp.tile([P, w * P], U32, tag="cq", name="cq%d_%d" % (u, n), align_bytes=64)
             sq = qp.tile([P, w * P], U8, tag="sq", name="sq%d_%d" % (u, n), align_bytes=64)
-            nc.vector.quantize_mx(out=cq[:].bitcast(FP8X4), scales=sq[:], in_=g[:].bitcast(BF16))
+            nc.vector.quantize_mx(out=cq[:].bitcast(FP8X4), scales=sq[:], in_=gs[u, n][:].bitcast(BF16))
             for b in range(w):
                 blk[r0 + 4 * n + b] = (cq, sq, b)
 
@@ -211,45 +230,75 @@ def tile_predictor_pa_t_kernel(tc, x, W1, b1, out):
             nc.sync.dma_start(out=ov[:, r * C:(r + size) * C], in_=o[:, b * C:(b + size) * C])
 
         n_units = len(UNITS)
-        for p in range(n_units + 1):
+        swaps = {u: exchange(u) for u in range(n_units)}
+
+        def swap(u, k):
+            if u < n_units:
+                swaps[u](k)
+
+        for k in range(3):
+            swap(0, k)
+        transpose(0)
+        leave(0, 0, nc.scalar.copy)
+        pw = [multiply_w(k) for k in range(TAPS)]
+        swap(1, 0)
+        nc.vector.tensor_copy(out=wg[:, 0], in_=pw[0][:].rearrange("p t c -> p c t"))
+        swap(1, 1)
+        quantise(0, 0)
+        swap(1, 2)
+        for k in (1, 2):
+            nc.scalar.copy(out=wg[:, k], in_=pw[k][:].rearrange("p t c -> p c t"))
+        transpose(1)
+        swap(2, 0)
+        quantise_w(0)
+        swap(2, 1)
+        quantise_w(1)
+        swap(2, 2)
+        quantise_w(2)
+        leave(1, 0, nc.scalar.copy)
+        leave(1, 1, nc.vector.tensor_copy)
+        transpose(2)
+        pbias = psum.tile([P, TAPS, C], F32, tag="b3", name="pbias")
+        for k in range(TAPS):
+            nc.tensor.matmul(out=pbias[:, k, :], lhsT=coef[:, k, :], rhs=bz[:], start=True, stop=True)
+        swap(3, 0)
+        quantise(1, 0)
+        swap(3, 1)
+        leave(2, 0, nc.scalar.copy)
+        leave(2, 1, nc.scalar.copy)
+        nc.vector.tensor_copy(out=bias[:], in_=pbias[:])
+        swap(3, 2)
+        waiting = multiply(1, [4])
+        quantise(2, 0)
+        swap(4, 0)
+
+        for p in range(3, n_units + 1):
             last = p == n_units
-            late = []
             if not last:
-                if p + 1 < n_units:
-                    order_words(p + 1)
-                gs = transpose_and_leave(p)
-                if p == 0:
-                    prepare_w()
-                if p == 1:
-                    pbias = psum.tile([P, TAPS, C], F32, tag="b3", name="pbias")
-                    for k in range(TAPS):
-                        nc.tensor.matmul(out=pbias[:, k, :], lhsT=coef[:, k, :], rhs=bz[:], start=True, stop=True)
-                for n, g in enumerate(gs):
-                    if n == 3:
-                        late.append((n, g))
-                    else:
-                        quantise(p, n, g)
-                if p == 1:
-                    nc.vector.tensor_copy(out=bias[:], in_=pbias[:])
-            banks = []
-            if p >= 2:
-                nb = UNITS[p - 1][1]
-                banks = multiply(p - 1, [4, 2, 2] if last else [4] * (nb // 4))
-            if not last:
-                for n, (pb, r, size) in enumerate(banks):
+                transpose(p)
+                for h in range(UNITS[p][1] // 2):
+                    leave(p, h, nc.scalar.copy)
+                for pb, r, size in waiting:
                     add_bias(pb, r, size)
-                    if n == 0:
-                        for m, g in late:
-                            quantise(p, m, g)
-                        late = []
-                for m, g in late:
-                    quantise(p, m, g)
-            if p >= 3:
-                r0, nb = UNITS[p - 2]
-                piece = 4 if last else min(nb, 8)
-                for r in range(r0, r0 + nb, piece):
-                    tanh_store(r, piece)
-                    load_next()
+                waiting = []
+                swap(p + 1, 1)
+                quantise(p, 0)
+                swap(p + 1, 2)
+                for n in range(1, UNITS[p][1] // 4):
+                    quantise(p, n)
+                swap(p + 2, 0)
+            banks = multiply(p - 1, [4, 2, 2] if last else [4] * (UNITS[p - 1][1] // 4))
+            if not last:
+                for pb, r, size in banks[:-1]:
+                    add_bias(pb, r, size)
+            for pb, r, size in waiting if last else []:
+                add_bias(pb, r, size)
+            if not last:
+                waiting = banks[-1:]
+            r0, nb = UNITS[p - 2]
+            piece = 4 if last else min(nb, 8)
+            for r in range(r0, r0 + nb, piece):
+                tanh_store(r, piece)
             if last:
                 for pb, r, size in banks:
                     add_bias(pb, r, size)

@@ -242,11 +242,10 @@ def tile_predictor_pa_t_kernel(tc, x, W1, b1, out):
         leave(0, 0, nc.scalar.copy)
         pw = [multiply_w(k) for k in range(TAPS)]
         swap(1, 0)
-        nc.vector.tensor_copy(out=wg[:, 0], in_=pw[0][:].rearrange("p t c -> p c t"))
         swap(1, 1)
         quantise(0, 0)
         swap(1, 2)
-        for k in (1, 2):
+        for k in range(TAPS):
             nc.scalar.copy(out=wg[:, k], in_=pw[k][:].rearrange("p t c -> p c t"))
         transpose(1)
         swap(2, 0)
@@ -256,7 +255,7 @@ def tile_predictor_pa_t_kernel(tc, x, W1, b1, out):
         swap(2, 2)
         quantise_w(2)
         leave(1, 0, nc.scalar.copy)
-        leave(1, 1, nc.vector.tensor_copy)
+        leave(1, 1, nc.scalar.copy)
         transpose(2)
         pbias = psum.tile([P, TAPS, C], F32, tag="b3", name="pbias")
         for k in range(TAPS):
@@ -266,7 +265,7 @@ def tile_predictor_pa_t_kernel(tc, x, W1, b1, out):
         swap(3, 1)
         leave(2, 0, nc.scalar.copy)
         leave(2, 1, nc.scalar.copy)
-        nc.vector.tensor_copy(out=bias[:], in_=pbias[:])
+        nc.scalar.copy(out=bias[:], in_=pbias[:])
         swap(3, 2)
         waiting = multiply(1, [4])
         quantise(2, 0)
@@ -278,28 +277,23 @@ def tile_predictor_pa_t_kernel(tc, x, W1, b1, out):
                 transpose(p)
                 for h in range(UNITS[p][1] // 2):
                     leave(p, h, nc.scalar.copy)
-                for pb, r, size in waiting:
-                    add_bias(pb, r, size)
-                waiting = []
-                swap(p + 1, 1)
-                quantise(p, 0)
-                swap(p + 1, 2)
-                for n in range(1, UNITS[p][1] // 4):
-                    quantise(p, n)
-                swap(p + 2, 0)
-            banks = multiply(p - 1, [4, 2, 2] if last else [4] * (UNITS[p - 1][1] // 4))
-            if not last:
-                for pb, r, size in banks[:-1]:
-                    add_bias(pb, r, size)
-            for pb, r, size in waiting if last else []:
+            ahead = [lambda: swap(p + 1, 1), lambda: swap(p + 1, 2)]
+            for n, (pb, r, size) in enumerate(waiting):
                 add_bias(pb, r, size)
+                ahead[n]()
+            for step in ahead[len(waiting):]:
+                step()
             if not last:
-                waiting = banks[-1:]
+                for n in range(UNITS[p][1] // 4):
+                    quantise(p, n)
+                    if n == 0:
+                        swap(p + 2, 0)
+            waiting = multiply(p - 1, [4, 2, 2] if last else [4] * (UNITS[p - 1][1] // 4))
             r0, nb = UNITS[p - 2]
             piece = 4 if last else min(nb, 8)
             for r in range(r0, r0 + nb, piece):
                 tanh_store(r, piece)
             if last:
-                for pb, r, size in banks:
+                for pb, r, size in waiting:
                     add_bias(pb, r, size)
                     tanh_store(r, size)

@@ -45,9 +45,9 @@ def tile_predictor_pa_t_kernel(tc, x, W1, b1, out):
         def load_next():
             r0, nb = LOADS[state["load"]]
             if state["load"] == 0:
-                t = const.tile([P, nb * E], BF16, name="rawh")
+                t = const.tile([P, nb * E], BF16, name="rawh", align_bytes=256)
             else:
-                t = rawp.tile([P, nb * E], BF16, name="raw%d" % r0)
+                t = rawp.tile([P, nb * E], BF16, name="raw%d" % r0, align_bytes=256)
             state["load"] += 1
             nc.sync.dma_start(out=t[:], in_=xv[:, r0 * E:(r0 + nb) * E])
             for b in range(nb):
@@ -58,7 +58,7 @@ def tile_predictor_pa_t_kernel(tc, x, W1, b1, out):
             state[kind] += 1
             return t
 
-        ident = const.tile([P, P], F32, name="ident")
+        ident = const.tile([P, P], F32, name="ident", align_bytes=256)
         make_identity(nc, ident[:])
         warm = const.tile([P, 1], F32, name="warm")
         nc.vector.memset(warm[:], 0.0)
@@ -70,7 +70,7 @@ def tile_predictor_pa_t_kernel(tc, x, W1, b1, out):
         nc.vector.memset(coef[:], 3.0)
         nc.vector.memset(coef[0:1, 0, 0:1], 1.0)
         nc.vector.memset(coef[0:1, 1, 0:1], 2.0)
-        shift = const.tile([P, P], F32, name="shift")
+        shift = const.tile([P, P], F32, name="shift", align_bytes=256)
         nc.vector.memset(shift[:], 0.0)
         nc.vector.tensor_copy(out=shift[:, 1:P], in_=ident[:, 0:P - 1])
 
@@ -92,10 +92,10 @@ def tile_predictor_pa_t_kernel(tc, x, W1, b1, out):
                     in_=ident[:].rearrange("q (h m v j) -> q m h v j", h=2, m=8, v=2)[:, :, :, v, :],
                 )
 
-        wg = const.tile([P, TAPS, C, 4], BF16, name="wg", align_bytes=64)
-        wq = const.tile([P, TAPS * C], U32, name="wq", align_bytes=64)
-        ws = const.tile([P, TAPS * C], U8, name="ws", align_bytes=64)
-        bias = const.tile([P, TAPS, C], F32, name="bias")
+        wg = const.tile([P, TAPS, C, 4], BF16, name="wg", align_bytes=256)
+        wq = const.tile([P, TAPS * C], U32, name="wq", align_bytes=256)
+        ws = const.tile([P, TAPS * C], U8, name="ws", align_bytes=256)
+        bias = const.tile([P, TAPS, C], F32, name="bias", align_bytes=256)
 
         def multiply_w(k):
             pw = psum.tile([P, 4, C], F32, tag="b%d" % k, name="pw%d" % k)
@@ -136,7 +136,7 @@ def tile_predictor_pa_t_kernel(tc, x, W1, b1, out):
             for t, i, n in parts:
                 runs = t[:, i * E:(i + n) * E].bitcast(F32).rearrange("p (n h m v i) -> p n h m v i", h=2, m=8, v=2, i=8)
                 low, high = runs[:, :, 0, :, 1, :], runs[:, :, 1, :, 0, :]
-                aside = tmpp.tile([P, n, 8, 8], F32, tag="aside", name="aside%d_%d" % (u, i))
+                aside = tmpp.tile([P, n, 8, 8], F32, tag="aside", name="aside%d_%d" % (u, i), align_bytes=256)
                 steps[0].append((aside[:], low))
                 steps[1].append((low, high))
                 steps[2].append((high, aside[:]))
@@ -168,7 +168,7 @@ def tile_predictor_pa_t_kernel(tc, x, W1, b1, out):
         def leave(u, h, copy):
             nb = UNITS[u][1]
             if h % 2 == 0:
-                gs[u, h // 2] = grp.tile([P, min(nb, 4) * 2 * P], F32, tag="g", name="g%d_%d" % (u, h), align_bytes=64)
+                gs[u, h // 2] = grp.tile([P, min(nb, 4) * 2 * P], F32, tag="g", name="g%d_%d" % (u, h), align_bytes=256)
             copy(
                 out=gs[u, h // 2][:, (h % 2) * 512:(h % 2 + 1) * 512].rearrange("p (b j v) -> p b j v", b=2, v=2),
                 in_=pas[u, h][:].rearrange("p (b v j) -> p b j v", b=2, v=2),
@@ -177,8 +177,8 @@ def tile_predictor_pa_t_kernel(tc, x, W1, b1, out):
         def quantise(u, n):
             r0, nb = UNITS[u]
             w = min(nb, 4)
-            cq = qp.tile([P, w * P], U32, tag="cq", name="cq%d_%d" % (u, n), align_bytes=64)
-            sq = qp.tile([P, w * P], U8, tag="sq", name="sq%d_%d" % (u, n), align_bytes=64)
+            cq = qp.tile([P, w * P], U32, tag="cq", name="cq%d_%d" % (u, n), align_bytes=256)
+            sq = qp.tile([P, w * P], U8, tag="sq", name="sq%d_%d" % (u, n), align_bytes=256)
             nc.vector.quantize_mx(out=cq[:].bitcast(FP8X4), scales=sq[:], in_=gs[u, n][:].bitcast(BF16))
             for b in range(w):
                 blk[r0 + 4 * n + b] = (cq, sq, b)
@@ -212,7 +212,7 @@ def tile_predictor_pa_t_kernel(tc, x, W1, b1, out):
 
         def add_bias(pb, r, size):
             if r % 8 == 0 or r not in o_of:
-                o = outp.tile([P, 8 * C], F32, tag="o", name="o%d" % r)
+                o = outp.tile([P, 8 * C], F32, tag="o", name="o%d" % r, align_bytes=256)
                 for b in range(8):
                     o_of[r + b] = (o, b)
             o, b = o_of[r]

from contextlib import ExitStack

import concourse.mybir as mybir
from concourse.masks import make_identity

F32 = mybir.dt.float32
BF16 = mybir.dt.bfloat16
U32 = mybir.dt.uint32
U8 = mybir.dt.uint8
FP8X4 = mybir.dt.float8_e4m3fn_x4
ADD = mybir.AluOpType.add
TANH = mybir.ActivationFunctionType.Tanh

P = 128
N_ROWS = 16384
E = 512
C = 128
TAPS = 3
R = N_ROWS // P
WORDS = E // 2
FLOPS = 2 * N_ROWS * E * C * TAPS

UNITS = [(-2, 2), (0, 4), (4, 4)] + [(r, 8) for r in range(8, R, 8)]
LOADS = [(R - 2, 2), (0, 4), (4, 4)] + [(r, 8) for r in range(8, R - 8, 8)] + [(R - 8, 6)]


def tile_predictor_pa_t_kernel(tc, x, W1, b1, out):
    nc = tc.nc
    xv = x.rearrange("(j r) k -> j (r k)", r=R)
    ov = out.rearrange("(j r) c -> j (r c)", r=R)
    with ExitStack() as ctx:
        const = ctx.enter_context(tc.tile_pool(name="const", bufs=1))
        rawp = ctx.enter_context(tc.tile_pool(name="raw", bufs=1))
        tmpp = ctx.enter_context(tc.tile_pool(name="aside", bufs=2))
        grp = ctx.enter_context(tc.tile_pool(name="grouped", bufs=4))
        qp = ctx.enter_context(tc.tile_pool(name="quant", bufs=8))
        outp = ctx.enter_context(tc.tile_pool(name="outs", bufs=12))
        psum = ctx.enter_context(tc.psum_pool(name="psum", bufs=1))
        ctx.enter_context(tc.manual_schedule())

        raw_of = {}
        blk = {}
        state = {"a": 0, "b": 0, "load": 0}

        def load_next():
            r0, nb = LOADS[state["load"]]
            if state["load"] == 0:
                t = const.tile([P, nb * E], BF16, name="rawh", align_bytes=256)
            else:
                t = rawp.tile([P, nb * E], BF16, name="raw%d" % r0, align_bytes=256)
            state["load"] += 1
            nc.sync.dma_start(out=t[:], in_=xv[:, r0 * E:(r0 + nb) * E])
            for b in range(nb):
                raw_of[r0 + b] = (t, b)

        def psum_bank(kind):
            t = psum.tile([P, 512], F32, tag="%s%d" % (kind, state[kind] % 4), name="p%s%d" % (kind, state[kind]))
            state[kind] += 1
            return t

        ident = const.tile([P, P], F32, name="ident", align_bytes=256)
        make_identity(nc, ident[:])
        warm = const.tile([P, 1], F32, name="warm")
        nc.vector.memset(warm[:], 0.0)
        nc.scalar.activation(out=warm[:], in_=warm[:], func=TANH)
        bz = const.tile([P, C], BF16, name="bz")
        nc.vector.memset(bz[:], 0.0)
        nc.scalar.dma_start(out=bz[0:1, :], in_=b1)
        coef = const.tile([P, TAPS, P], BF16, name="coef")
        nc.vector.memset(coef[:], 3.0)
        nc.vector.memset(coef[0:1, 0, 0:1], 1.0)
        nc.vector.memset(coef[0:1, 1, 0:1], 2.0)
        shift = const.tile([P, P], F32, name="shift", align_bytes=256)
        nc.vector.memset(shift[:], 0.0)
        nc.vector.tensor_copy(out=shift[:, 1:P], in_=ident[:, 0:P - 1])

        load_next()
        wraw = const.tile([P, TAPS, 4, C], BF16, name="wraw")
        nc.sync.dma_start(
            out=wraw[:].rearrange("p k (u e) c -> p k u (e c)", u=2),
            in_=W1.rearrange("k (p u e) c -> p k u (e c)", u=2, p=P, e=2),
        )
        while state["load"] < len(LOADS):
            load_next()

        perm = const.tile([P, 2, 2, P], BF16, name="perm")
        nc.vector.memset(perm[:], 0.0)
        for v in range(2):
            for s in range(2):
                nc.vector.tensor_copy(
                    out=perm[:, v, s, :].rearrange("q (m h j z) -> q m h j z", m=8, h=2, z=2)[:, :, :, :, s],
                    in_=ident[:].rearrange("q (h m v j) -> q m h v j", h=2, m=8, v=2)[:, :, :, v, :],
                )

        wg = const.tile([P, TAPS, C, 4], BF16, name="wg", align_bytes=256)
        wq = const.tile([P, TAPS * C], U32, name="wq", align_bytes=256)
        ws = const.tile([P, TAPS * C], U8, name="ws", align_bytes=256)
        bias = const.tile([P, TAPS, C], F32, name="bias", align_bytes=256)

        def multiply_w(k):
            pw = psum.tile([P, 4, C], F32, tag="b%d" % k, name="pw%d" % k)
            for v in range(2):
                for e in range(2):
                    for s in range(2):
                        nc.tensor.matmul(
                            out=pw[:, 2 * v + e, :],
                            lhsT=perm[:, v, s, :],
                            rhs=wraw[:, k, 2 * s + e, :],
                            start=(s == 0),
                            stop=(s == 1),
                        )
            return pw

        def quantise_w(k):
            nc.vector.quantize_mx(
                out=wq[:, k * C:(k + 1) * C].bitcast(FP8X4),
                scales=ws[:, k * C:(k + 1) * C],
                in_=wg[:, k].rearrange("p c t -> p (c t)"),
            )

        done = set()

        def exchange(u):
            r0, nb = UNITS[u]
            parts = []
            for r in range(r0, r0 + nb):
                t, i = raw_of[r % R]
                if r % R in done:
                    continue
                done.add(r % R)
                if parts and parts[-1][0] is t:
                    parts[-1][2] += 1
                else:
                    parts.append([t, i, 1])
            steps = [[], [], []]
            for t, i, n in parts:
                runs = t[:, i * E:(i + n) * E].bitcast(F32).rearrange("p (n h m v i) -> p n h m v i", h=2, m=8, v=2, i=8)
                low, high = runs[:, :, 0, :, 1, :], runs[:, :, 1, :, 0, :]
                aside = tmpp.tile([P, n, 8, 8], F32, tag="aside", name="aside%d_%d" % (u, i), align_bytes=256)
                steps[0].append((aside[:], low))
                steps[1].append((low, high))
                steps[2].append((high, aside[:]))

            def step(k):
                for dst, src in steps[k]:
                    nc.vector.tensor_copy(out=dst, in_=src)

            return step

        pas = {}
        gs = {}

        def transpose(u):
            r0, nb = UNITS[u]
            for h in range(nb // 2):
                pa = psum_bank("a")
                pas[u, h] = pa
                for b in range(2):
                    t, i = raw_of[(r0 + 2 * h + b) % R]
                    for v in range(2):
                        lo = i * WORDS + v * P
                        nc.tensor.transpose(
                            pa[:, (2 * b + v) * P:(2 * b + v + 1) * P],
                            t[:].bitcast(F32)[:, lo:lo + P],
                            (shift if r0 < 0 else ident)[:],
                        )

        def leave(u, h, copy):
            nb = UNITS[u][1]
            if h % 2 == 0:
                gs[u, h // 2] = grp.tile([P, min(nb, 4) * 2 * P], F32, tag="g", name="g%d_%d" % (u, h), align_bytes=256)
            copy(
                out=gs[u, h // 2][:, (h % 2) * 512:(h % 2 + 1) * 512].rearrange("p (b j v) -> p b j v", b=2, v=2),
                in_=pas[u, h][:].rearrange("p (b v j) -> p b j v", b=2, v=2),
            )

        def quantise(u, n):
            r0, nb = UNITS[u]
            w = min(nb, 4)
            cq = qp.tile([P, w * P], U32, tag="cq", name="cq%d_%d" % (u, n), align_bytes=256)
            sq = qp.tile([P, w * P], U8, tag="sq", name="sq%d_%d" % (u, n), align_bytes=256)
            nc.vector.quantize_mx(out=cq[:].bitcast(FP8X4), scales=sq[:], in_=gs[u, n][:].bitcast(BF16))
            for b in range(w):
                blk[r0 + 4 * n + b] = (cq, sq, b)

        def multiply(u, sizes):
            r0, nb = UNITS[u]
            banks = []
            r = r0
            for n, size in enumerate(sizes):
                pb = psum_bank("b" if n < 4 else "a")
                passes = [(r + h, 0, 2, h) for h in range(0, size, 2)]
                passes += [(r + h - 1, 1, 2, h) for h in range(0, size, 2)]
                for h in range(0, size, 2):
                    passes += [(r + h - 2, 2, 1, h), (r + h + 1, 0, 1, h + 1)]
                for m, (s, k, nk, ob) in enumerate(passes):
                    cq, sq, i = blk[s]
                    nc.tensor.matmul_mx(
                        out=pb[:, ob * C:(ob + nk) * C],
                        lhsT=cq[:, i * P:(i + 1) * P].bitcast(FP8X4),
                        lhsT_scale=sq[:, i * P:(i + 1) * P],
                        rhs=wq[:, k * C:(k + nk) * C].bitcast(FP8X4),
                        rhs_scale=ws[:, k * C:(k + nk) * C],
                        start=(m == 0),
                        stop=(m == len(passes) - 1),
                    )
                banks.append((pb, r, size))
                r += size
            return banks

        o_of = {}

        def add_bias(pb, r, size):
            if r % 8 == 0 or r not in o_of:
                o = outp.tile([P, 8 * C], F32, tag="o", name="o%d" % r, align_bytes=256)
                for b in range(8):
                    o_of[r + b] = (o, b)
            o, b = o_of[r]
            ob = o[:, b * C:(b + size) * C].rearrange("p (n c) -> p n c", c=C)
            pv = pb[:, 0:size * C].rearrange("p (n c) -> p n c", c=C)
            if r == 0:
                nc.vector.tensor_tensor(out=ob[:, 0:3, :], in0=pv[:, 0:3, :], in1=bias[:], op=ADD)
                nc.vector.tensor_tensor(out=ob[:, 3, :], in0=pv[:, 3, :], in1=bias[:, 2, :], op=ADD)
            else:
                nc.vector.tensor_tensor(out=ob, in0=pv, in1=bias[:, 2:3, :].to_broadcast([P, size, C]), op=ADD)

        def tanh_store(r, size):
            o, b = o_of[r]
            nc.scalar.activation(out=o[:, b * C:(b + size) * C], in_=o[:, b * C:(b + size) * C], func=TANH)
            nc.sync.dma_start(out=ov[:, r * C:(r + size) * C], in_=o[:, b * C:(b + size) * C])

        n_units = len(UNITS)
        swaps = {u: exchange(u) for u in range(n_units)}

        def swap(u, k):
            if u < n_units:
                swaps[u](k)

        for k in range(3):
            swap(0, k)
        transpose(0)
        leave(0, 0, nc.scalar.copy)
        pw = [multiply_w(k) for k in range(TAPS)]
        swap(1, 0)
        swap(1, 1)
        quantise(0, 0)
        swap(1, 2)
        for k in range(TAPS):
            nc.scalar.copy(out=wg[:, k], in_=pw[k][:].rearrange("p t c -> p c t"))
        transpose(1)
        swap(2, 0)
        quantise_w(0)
        swap(2, 1)
        quantise_w(1)
        swap(2, 2)
        quantise_w(2)
        leave(1, 0, nc.scalar.copy)
        leave(1, 1, nc.scalar.copy)
        transpose(2)
        pbias = psum.tile([P, TAPS, C], F32, tag="b3", name="pbias")
        for k in range(TAPS):
            nc.tensor.matmul(out=pbias[:, k, :], lhsT=coef[:, k, :], rhs=bz[:], start=True, stop=True)
        swap(3, 0)
        quantise(1, 0)
        swap(3, 1)
        leave(2, 0, nc.scalar.copy)
        leave(2, 1, nc.scalar.copy)
        nc.scalar.copy(out=bias[:], in_=pbias[:])
        swap(3, 2)
        waiting = multiply(1, [4])
        quantise(2, 0)
        swap(4, 0)

        for p in range(3, n_units + 1):
            last = p == n_units
            if not last:
                transpose(p)
                for h in range(UNITS[p][1] // 2):
                    leave(p, h, nc.scalar.copy)
            ahead = [lambda: swap(p + 1, 1), lambda: swap(p + 1, 2)]
            for n, (pb, r, size) in enumerate(waiting):
                add_bias(pb, r, size)
                ahead[n]()
            for step in ahead[len(waiting):]:
                step()
            if not last:
                for n in range(UNITS[p][1] // 4):
                    quantise(p, n)
                    if n == 0:
                        swap(p + 2, 0)
            waiting = multiply(p - 1, [4, 2, 2] if last else [4] * (UNITS[p - 1][1] // 4))
            r0, nb = UNITS[p - 2]
            piece = 4 if last else min(nb, 8)
            for r in range(r0, r0 + nb, piece):
                tanh_store(r, piece)
            if last:
                for pb, r, size in waiting:
                    add_bias(pb, r, size)
                    tanh_store(r, size)
